import numpy as np
import ml_dtypes


def mxq(x, axis, fmt="e4m3"):
    dtype, down = {"e4m3": (ml_dtypes.float8_e4m3fn, 7), "e5m2": (ml_dtypes.float8_e5m2, 14)}[fmt]
    v = np.moveaxis(np.asarray(x, np.float32).astype(ml_dtypes.bfloat16).astype(np.float64), axis, -1)
    blocks = v.reshape(v.shape[:-1] + (-1, 32))
    amax = np.abs(blocks).max(-1, keepdims=True)
    byte = np.maximum(np.where(amax > 0, np.frexp(amax)[1] - 1 + 127, 0) - down, 1)
    scale = np.exp2(byte - 127.0)
    codes = (blocks / scale).astype(np.float32).astype(dtype).astype(np.float64)
    return np.moveaxis((codes * scale).reshape(v.shape), -1, axis)


WIDE = False


def mx_kscale(k):
    if not WIDE:
        return np.ones(k)
    levels = np.array([10, -10, 5, -5, 0])
    a = np.random.permutation(np.resize(levels, k // 512 * 4)).reshape(k // 512, 4)
    idx = np.arange(k)
    return np.exp2(a[idx // 512, idx % 128 // 32])


BF16 = ml_dtypes.bfloat16


def bf(x):
    return np.asarray(x, np.float32).astype(BF16)


def f64(x):
    return np.asarray(x).astype(np.float64)


B, S, D, C = 8, 1024, 256, 512
GAMMA = 0.96875


def decay_mask(i, j):
    diff = f64(i[:, None] - j[None, :])
    return np.where(diff >= 0, np.exp(diff * np.log(GAMMA)), 0.0)


def setup_inputs():
    s = mx_kscale(S)
    return {"q": bf(np.random.standard_normal((B, S, D)) / D**0.25),
            "k": bf(np.random.standard_normal((B, S, D)) / D**0.25 * s[:, None]),
            "v": bf(np.random.standard_normal((B, S, D)) / s[:, None])}


def reference(q, k, v):
    qf, kf = f64(q), f64(k)
    vq = mxq(f64(v), 1, "e4m3")
    pos = np.arange(S)
    out = []
    for r in range(0, S, C):
        e = r + C
        scores = (qf[:, r:e] @ kf[:, :e].transpose(0, 2, 1)) * decay_mask(pos[r:e], pos[:e])
        out.append(mxq(scores, 2, "e4m3") @ vq[:, :e])
    return np.concatenate(out, 1)

@@ -1,0 +1,229 @@
+import math
+from contextlib import ExitStack
+
+import concourse.masks as masks
+import concourse.mybir as mybir
+
+F32 = mybir.dt.float32
+BF16 = mybir.dt.bfloat16
+I32 = mybir.dt.int32
+U32 = mybir.dt.uint32
+U8 = mybir.dt.uint8
+FP8X4 = mybir.dt.float8_e4m3fn_x4
+MULT = mybir.AluOpType.mult
+IS_GE = mybir.AluOpType.is_ge
+EXP = mybir.ActivationFunctionType.Exp
+
+B, S, D = 8, 1024, 256
+P = 128
+PACK = 4
+KG = P * PACK
+LN_GAMMA = math.log(0.96875)
+FLOPS = 2 * 2 * D * 3 * KG * KG * B
+
+MANUAL = True
+MX_LAG = 3
+
+UNITS = [(0, 0), (1, 0), (2, 0), (3, 0), (4, 0), (4, 1), (5, 0), (5, 1), (6, 0), (6, 1), (7, 0), (7, 1)]
+NU = len(UNITS)
+
+
+def tile_retention_pa_t_kernel(tc, q, k, v, out):
+    nc = tc.nc
+    with ExitStack() as ctx:
+        const = ctx.enter_context(tc.tile_pool(name="const", bufs=1))
+        inputs = ctx.enter_context(tc.tile_pool(name="inputs", bufs=1))
+        flipped = ctx.enter_context(tc.tile_pool(name="flipped", bufs=2))
+        work = ctx.enter_context(tc.tile_pool(name="work", bufs=3))
+        packed = ctx.enter_context(tc.tile_pool(name="packed", bufs=6))
+        vpool = ctx.enter_context(tc.tile_pool(name="vpool", bufs=2))
+        stage = ctx.enter_context(tc.tile_pool(name="stage", bufs=16))
+        tp = ctx.enter_context(tc.psum_pool(name="tp", bufs=2))
+        sc = ctx.enter_context(tc.psum_pool(name="sc", bufs=4))
+        op = ctx.enter_context(tc.psum_pool(name="op", bufs=2))
+        if MANUAL:
+            ctx.enter_context(tc.manual_schedule())
+
+        q_sb, k_sb, v_sb = {}, {}, {}
+        for b in range(B):
+            for g in range(2):
+                rows = slice(KG * g, KG * g + KG)
+                q_sb[b, g] = inputs.tile([P, PACK * D], BF16, name="q%d_%d" % (b, g))
+                nc.sync.dma_start(out=q_sb[b, g][:], in_=q[b, rows, :].rearrange("(p n) d -> p (n d)", n=PACK))
+                k_sb[b, g] = inputs.tile([P, PACK * D], BF16, name="k%d_%d" % (b, g))
+                nc.sync.dma_start(out=k_sb[b, g][:], in_=k[b, rows, :].rearrange("(p n) d -> p (n d)", n=PACK))
+                v_sb[b, g] = inputs.tile([P, PACK, D], BF16, name="v%d_%d" % (b, g))
+                nc.sync.dma_start(out=v_sb[b, g][:], in_=v[b, rows, :].rearrange("(t p) d -> p t d", p=P))
+
+        xi = const.tile([P, P * PACK], I32, name="xi")
+        nc.gpsimd.iota(out=xi[:], pattern=[[1, P], [-P, PACK]], base=P * (PACK - 1), channel_multiplier=-1)
+        ident = const.tile([P, P], F32, name="ident")
+        masks.make_identity(nc, ident[:])
+        xf = const.tile([P, P, PACK], F32, name="xf")
+        nc.vector.tensor_copy(out=xf[:].rearrange("p c m -> p (c m)"), in_=xi[:])
+        gz = []
+        for delta in range(3):
+            z = const.tile([P, P, PACK], BF16, name="gz%d" % delta, align_bytes=64)
+            nc.vector.memset(z[:].rearrange("p c t -> p (c t)").bitcast(I32), 0)
+            gz.append(z)
+        near = const.tile([P, P, PACK], F32, name="near")
+        far = const.tile([P, P, 2 * PACK], F32, name="far")
+
+        def make_near():
+            nc.scalar.activation(out=near[:], in_=xf[:], func=EXP, bias=0.0, scale=LN_GAMMA)
+            nc.vector.scalar_tensor_tensor(
+                out=near[:, :, PACK - 1],
+                in0=xf[:, :, PACK - 1],
+                scalar=0.0,
+                in1=near[:, :, PACK - 1],
+                op0=IS_GE,
+                op1=MULT,
+            )
+
+        def make_far():
+            for half in range(2):
+                nc.scalar.activation(
+                    out=far[:, :, PACK * half : PACK * half + PACK],
+                    in_=xf[:],
+                    func=EXP,
+                    bias=(1 - half) * KG * LN_GAMMA,
+                    scale=LN_GAMMA,
+                )
+
+        qT, kT = {}, {}
+
+        def flip(b, g):
+            for src, dst, tag in ((q_sb, qT, "qT%d" % g), (k_sb, kT, "kT%d" % g)):
+                bank = tp.tile([P, PACK, P], F32, tag="tp", name="tpbank")
+                words = src[b, g][:].bitcast(F32)
+                for n in range(PACK):
+                    nc.tensor.transpose(bank[:, n, :], words[:, P * n : P * n + P], ident[:])
+                t = flipped.tile([P, KG, 2], BF16, tag=tag, name=tag)
+                nc.scalar.copy(
+                    out=t[:].rearrange("w s e -> w (s e)").bitcast(F32).rearrange("w (p n) -> w p n", n=PACK),
+                    in_=bank[:].rearrange("w n p -> w p n"),
+                )
+                dst[b, g] = t
+
+        vg, vc, vs = {}, {}, {}
+
+        def v_regroup(b, g):
+            t = vpool.tile([P, D, PACK], BF16, tag="vg%d" % g, name="vg", align_bytes=64)
+            nc.scalar.copy(
+                out=t[:].rearrange("p (c i) t -> p c t i", i=4),
+                in_=v_sb[b, g][:].rearrange("p t (c i) -> p c t i", i=4),
+            )
+            vg[b, g] = t
+
+        def v_quantise(b, g):
+            vc[b, g] = vpool.tile([P, D], U32, tag="vc%d" % g, name="vc", align_bytes=64)
+            vs[b, g] = vpool.tile([P, D], U8, tag="vs%d" % g, name="vs", align_bytes=64)
+            nc.vector.quantize_mx(
+                out=vc[b, g][:].bitcast(FP8X4),
+                scales=vs[b, g][:],
+                in_=vg[b, g][:].rearrange("p d t -> p (d t)"),
+            )
+
+        seq = [(b, ib, g) for b in range(B) for (ib, g) in UNITS]
+        n_steps = len(seq)
+        banks, grouped, codes, planes, obank = {}, {}, {}, {}, {}
+
+        def scores(s, mid):
+            b, ib, g = seq[s]
+            nv = min(ib - PACK * g, PACK - 1) + 1
+            bank = sc.tile([P, PACK, P], F32, tag="sc", name="scbank")
+            cols = slice(P * (ib % PACK), P * (ib % PACK) + P)
+            for t in range(nv):
+                for e in range(2):
+                    nc.tensor.matmul(
+                        out=bank[:, t, :],
+                        lhsT=kT[b, g][:, P * t : P * t + P, e],
+                        rhs=qT[b, ib // PACK][:, cols, e],
+                        start=(e == 0),
+                        stop=(e == 1),
+                    )
+                if t == 0 and mid is not None:
+                    flip(mid[0], mid[1])
+            banks[s] = bank
+
+        def mask_mult(s):
+            b, ib, g = seq[s]
+            delta = ib - PACK * g
+            nv = min(delta, PACK - 1) + 1
+            if delta < PACK - 1:
+                t = gz[delta]
+            else:
+                t = work.tile([P, P, PACK], BF16, tag="grouped", name="grouped", align_bytes=64)
+            if delta < PACK:
+                weights = near[:, :, PACK - 1 - delta : PACK]
+            else:
+                weights = far[:, :, 2 * PACK - 1 - delta : 3 * PACK - 1 - delta]
+            nc.vector.tensor_tensor(
+                out=t[:, :, 0:nv],
+                in0=banks[s][:, 0:nv, :].rearrange("p t c -> p c t"),
+                in1=weights,
+                op=MULT,
+            )
+            grouped[s] = t
+
+        def quantise(s):
+            codes[s] = packed.tile([P, P], U32, tag="codes", name="codes", align_bytes=64)
+            planes[s] = packed.tile([P, P], U8, tag="planes", name="planes", align_bytes=64)
+            nc.vector.quantize_mx(
+                out=codes[s][:].bitcast(FP8X4),
+                scales=planes[s][:],
+                in_=grouped[s][:].rearrange("p c t -> p (c t)"),
+            )
+
+        def mx(s):
+            b, ib, g = seq[s]
+            h = ib // 2
+            if (b, h) not in obank:
+                obank[b, h] = op.tile([P, 2, D], F32, tag="op", name="opbank")
+            last = g == ib // PACK
+            nc.tensor.matmul_mx(
+                out=obank[b, h][:, ib % 2, :],
+                lhsT=codes[s][:].bitcast(FP8X4),
+                lhsT_scale=planes[s][:],
+                rhs=vc[b, g][:].bitcast(FP8X4),
+                rhs_scale=vs[b, g][:],
+                start=(g == 0),
+                stop=last,
+            )
+            if last and ib % 2 == 1:
+                o = stage.tile([P, 2, D], F32, tag="o", name="o")
+                nc.scalar.copy(out=o[:], in_=obank[b, h][:])
+                nc.sync.dma_start(
+                    out=out[b, 2 * P * h : 2 * P * h + 2 * P, :].rearrange("(n c) d -> c n d", c=P), in_=o[:]
+                )
+
+        flips, regroups, vquants = {}, {}, {}
+        flips[2] = (0, 1)
+        regroups[3] = (0, 1)
+        vquants[2] = (0, 0)
+        vquants[5] = (0, 1)
+        for b in range(1, B):
+            flips[NU * b - 6] = (b, 0)
+            flips[NU * b - 2] = (b, 1)
+            regroups[NU * b - 8] = (b, 0)
+            vquants[NU * b - 6] = (b, 0)
+            regroups[NU * b - 4] = (b, 1)
+            vquants[NU * b - 2] = (b, 1)
+
+        make_near()
+        flip(0, 0)
+        v_regroup(0, 0)
+        make_far()
+
+        for s in range(n_steps + MX_LAG):
+            if s < n_steps:
+                scores(s, flips.get(s))
+                mask_mult(s)
+            if 0 <= s - 1 < n_steps:
+                quantise(s - 1)
+            if s in vquants:
+                v_quantise(vquants[s][0], vquants[s][1])
+            if 0 <= s - MX_LAG < n_steps:
+                mx(s - MX_LAG)
+            if s in regroups:
+                v_regroup(regroups[s][0], regroups[s][1])

@@ -22,7 +22,8 @@ LN_GAMMA = math.log(0.96875)
 FLOPS = 2 * 2 * D * 3 * KG * KG * B
 
 MANUAL = True
-MX_LAG = 3
+MX_LAG = 6
+MX_RUN = 2
 
 UNITS = [(0, 0), (1, 0), (2, 0), (3, 0), (4, 0), (4, 1), (5, 0), (5, 1), (6, 0), (6, 1), (7, 0), (7, 1)]
 NU = len(UNITS)
@@ -35,7 +36,7 @@ def tile_retention_pa_t_kernel(tc, q, k, v, out):
         inputs = ctx.enter_context(tc.tile_pool(name="inputs", bufs=1))
         flipped = ctx.enter_context(tc.tile_pool(name="flipped", bufs=2))
         work = ctx.enter_context(tc.tile_pool(name="work", bufs=3))
-        packed = ctx.enter_context(tc.tile_pool(name="packed", bufs=6))
+        packed = ctx.enter_context(tc.tile_pool(name="packed", bufs=12))
         vpool = ctx.enter_context(tc.tile_pool(name="vpool", bufs=2))
         stage = ctx.enter_context(tc.tile_pool(name="stage", bufs=16))
         tp = ctx.enter_context(tc.psum_pool(name="tp", bufs=2))
@@ -55,6 +56,10 @@ def tile_retention_pa_t_kernel(tc, q, k, v, out):
                 v_sb[b, g] = inputs.tile([P, PACK, D], BF16, name="v%d_%d" % (b, g))
                 nc.sync.dma_start(out=v_sb[b, g][:], in_=v[b, rows, :].rearrange("(t p) d -> p t d", p=P))
 
+        cold = const.tile([P, 1], F32, name="cold")
+        warm = const.tile([P, 1], F32, name="warm")
+        nc.vector.memset(cold[:], 0.0)
+        nc.scalar.activation(out=warm[:], in_=cold[:], func=EXP, bias=0.0, scale=1.0)
         xi = const.tile([P, P * PACK], I32, name="xi")
         nc.gpsimd.iota(out=xi[:], pattern=[[1, P], [-P, PACK]], base=P * (PACK - 1), channel_multiplier=-1)
         ident = const.tile([P, P], F32, name="ident")
@@ -178,11 +183,13 @@ def tile_retention_pa_t_kernel(tc, q, k, v, out):
         def mx(s):
             b, ib, g = seq[s]
             h = ib // 2
-            if (b, h) not in obank:
-                obank[b, h] = op.tile([P, 2, D], F32, tag="op", name="opbank")
+            split = b == B - 1 and h == 3
+            key = (b, ib) if split else (b, 2 * h)
+            if key not in obank:
+                obank[key] = op.tile([P, 2, D], F32, tag="op", name="opbank")
             last = g == ib // PACK
             nc.tensor.matmul_mx(
-                out=obank[b, h][:, ib % 2, :],
+                out=obank[key][:, ib % 2, :],
                 lhsT=codes[s][:].bitcast(FP8X4),
                 lhsT_scale=planes[s][:],
                 rhs=vc[b, g][:].bitcast(FP8X4),
@@ -190,9 +197,13 @@ def tile_retention_pa_t_kernel(tc, q, k, v, out):
                 start=(g == 0),
                 stop=last,
             )
-            if last and ib % 2 == 1:
+            if last and split:
                 o = stage.tile([P, 2, D], F32, tag="o", name="o")
-                nc.scalar.copy(out=o[:], in_=obank[b, h][:])
+                nc.scalar.copy(out=o[:, 0, :], in_=obank[key][:, ib % 2, :])
+                nc.sync.dma_start(out=out[b, P * ib : P * ib + P, :], in_=o[:, 0, :])
+            elif last and ib % 2 == 1:
+                o = stage.tile([P, 2, D], F32, tag="o", name="o")
+                nc.scalar.copy(out=o[:], in_=obank[key][:])
                 nc.sync.dma_start(
                     out=out[b, 2 * P * h : 2 * P * h + 2 * P, :].rearrange("(n c) d -> c n d", c=P), in_=o[:]
                 )
@@ -215,6 +226,7 @@ def tile_retention_pa_t_kernel(tc, q, k, v, out):
         v_regroup(0, 0)
         make_far()
 
+        done = [0]
         for s in range(n_steps + MX_LAG):
             if s < n_steps:
                 scores(s, flips.get(s))
@@ -223,7 +235,9 @@ def tile_retention_pa_t_kernel(tc, q, k, v, out):
                 quantise(s - 1)
             if s in vquants:
                 v_quantise(vquants[s][0], vquants[s][1])
-            if 0 <= s - MX_LAG < n_steps:
-                mx(s - MX_LAG)
+            if s % MX_RUN == MX_RUN - 1 or s >= n_steps:
+                while done[0] <= s - MX_LAG and done[0] < n_steps:
+                    mx(done[0])
+                    done[0] += 1
             if s in regroups:
                 v_regroup(regroups[s][0], regroups[s][1])

@@ -23,7 +23,7 @@ FLOPS = 2 * 2 * D * 3 * KG * KG * B
 
 MANUAL = True
 MX_LAG = 6
-MX_RUN = 2
+MX_RUN = 4
 
 UNITS = [(0, 0), (1, 0), (2, 0), (3, 0), (4, 0), (4, 1), (5, 0), (5, 1), (6, 0), (6, 1), (7, 0), (7, 1)]
 NU = len(UNITS)
@@ -36,8 +36,8 @@ def tile_retention_pa_t_kernel(tc, q, k, v, out):
         inputs = ctx.enter_context(tc.tile_pool(name="inputs", bufs=1))
         flipped = ctx.enter_context(tc.tile_pool(name="flipped", bufs=2))
         work = ctx.enter_context(tc.tile_pool(name="work", bufs=3))
-        packed = ctx.enter_context(tc.tile_pool(name="packed", bufs=12))
-        vpool = ctx.enter_context(tc.tile_pool(name="vpool", bufs=2))
+        packed = ctx.enter_context(tc.tile_pool(name="packed", bufs=14))
+        vpool = ctx.enter_context(tc.tile_pool(name="vpool", bufs=3))
         stage = ctx.enter_context(tc.tile_pool(name="stage", bufs=16))
         tp = ctx.enter_context(tc.psum_pool(name="tp", bufs=2))
         sc = ctx.enter_context(tc.psum_pool(name="sc", bufs=4))
@@ -155,6 +155,12 @@ def tile_retention_pa_t_kernel(tc, q, k, v, out):
             b, ib, g = seq[s]
             delta = ib - PACK * g
             nv = min(delta, PACK - 1) + 1
+            if delta == 0:
+                lone = work.tile([P, P], BF16, tag="lone", name="lone")
+                nc.vector.tensor_tensor(out=lone[:], in0=banks[s][:, 0, :], in1=near[:, :, PACK - 1], op=MULT)
+                nc.scalar.copy(out=gz[0][:, :, 0], in_=lone[:])
+                grouped[s] = gz[0]
+                return
             if delta < PACK - 1:
                 t = gz[delta]
             else:
@@ -226,13 +232,18 @@ def tile_retention_pa_t_kernel(tc, q, k, v, out):
         v_regroup(0, 0)
         make_far()
 
+        def lonely(s):
+            return seq[s][1] == PACK * seq[s][2]
+
         done = [0]
         for s in range(n_steps + MX_LAG):
             if s < n_steps:
                 scores(s, flips.get(s))
                 mask_mult(s)
-            if 0 <= s - 1 < n_steps:
+            if 0 <= s - 1 < n_steps and not lonely(s - 1):
                 quantise(s - 1)
+            if 0 <= s - 3 < n_steps and lonely(s - 3):
+                quantise(s - 3)
             if s in vquants:
                 v_quantise(vquants[s][0], vquants[s][1])
             if s % MX_RUN == MX_RUN - 1 or s >= n_steps:

@@ -23,7 +23,7 @@ FLOPS = 2 * 2 * D * 3 * KG * KG * B
 
 MANUAL = True
 MX_LAG = 6
-MX_RUN = 4
+MX_RUN = 2
 
 UNITS = [(0, 0), (1, 0), (2, 0), (3, 0), (4, 0), (4, 1), (5, 0), (5, 1), (6, 0), (6, 1), (7, 0), (7, 1)]
 NU = len(UNITS)
@@ -36,8 +36,8 @@ def tile_retention_pa_t_kernel(tc, q, k, v, out):
         inputs = ctx.enter_context(tc.tile_pool(name="inputs", bufs=1))
         flipped = ctx.enter_context(tc.tile_pool(name="flipped", bufs=2))
         work = ctx.enter_context(tc.tile_pool(name="work", bufs=3))
-        packed = ctx.enter_context(tc.tile_pool(name="packed", bufs=14))
-        vpool = ctx.enter_context(tc.tile_pool(name="vpool", bufs=3))
+        packed = ctx.enter_context(tc.tile_pool(name="packed", bufs=12))
+        vpool = ctx.enter_context(tc.tile_pool(name="vpool", bufs=2))
         stage = ctx.enter_context(tc.tile_pool(name="stage", bufs=16))
         tp = ctx.enter_context(tc.psum_pool(name="tp", bufs=2))
         sc = ctx.enter_context(tc.psum_pool(name="sc", bufs=4))
@@ -103,11 +103,21 @@ def tile_retention_pa_t_kernel(tc, q, k, v, out):
                 words = src[b, g][:].bitcast(F32)
                 for n in range(PACK):
                     nc.tensor.transpose(bank[:, n, :], words[:, P * n : P * n + P], ident[:])
-                t = flipped.tile([P, KG, 2], BF16, tag=tag, name=tag)
-                nc.scalar.copy(
-                    out=t[:].rearrange("w s e -> w (s e)").bitcast(F32).rearrange("w (p n) -> w p n", n=PACK),
-                    in_=bank[:].rearrange("w n p -> w p n"),
-                )
+                if src is q_sb:
+                    t = flipped.tile([P, KG, 2], BF16, tag=tag, name=tag)
+                    nc.scalar.copy(
+                        out=t[:].rearrange("w s e -> w (s e)").bitcast(F32).rearrange("w (p n) -> w p n", n=PACK),
+                        in_=bank[:].rearrange("w n p -> w p n"),
+                    )
+                else:
+                    t = flipped.tile([P, 2, KG], BF16, tag=tag, name=tag)
+                    nc.scalar.copy(
+                        out=t[:].rearrange("w e (p n) -> w e p n", n=PACK),
+                        in_=bank[:]
+                        .rearrange("w n p -> w (n p)")
+                        .bitcast(BF16)
+                        .rearrange("w (n p e) -> w e p n", n=PACK, e=2),
+                    )
                 dst[b, g] = t
 
         vg, vc, vs = {}, {}, {}
@@ -142,7 +152,7 @@ def tile_retention_pa_t_kernel(tc, q, k, v, out):
                 for e in range(2):
                     nc.tensor.matmul(
                         out=bank[:, t, :],
-                        lhsT=kT[b, g][:, P * t : P * t + P, e],
+                        lhsT=kT[b, g][:, e, P * t : P * t + P],
                         rhs=qT[b, ib // PACK][:, cols, e],
                         start=(e == 0),
                         stop=(e == 1),
@@ -155,12 +165,6 @@ def tile_retention_pa_t_kernel(tc, q, k, v, out):
             b, ib, g = seq[s]
             delta = ib - PACK * g
             nv = min(delta, PACK - 1) + 1
-            if delta == 0:
-                lone = work.tile([P, P], BF16, tag="lone", name="lone")
-                nc.vector.tensor_tensor(out=lone[:], in0=banks[s][:, 0, :], in1=near[:, :, PACK - 1], op=MULT)
-                nc.scalar.copy(out=gz[0][:, :, 0], in_=lone[:])
-                grouped[s] = gz[0]
-                return
             if delta < PACK - 1:
                 t = gz[delta]
             else:
@@ -232,18 +236,13 @@ def tile_retention_pa_t_kernel(tc, q, k, v, out):
         v_regroup(0, 0)
         make_far()
 
-        def lonely(s):
-            return seq[s][1] == PACK * seq[s][2]
-
         done = [0]
         for s in range(n_steps + MX_LAG):
             if s < n_steps:
                 scores(s, flips.get(s))
                 mask_mult(s)
-            if 0 <= s - 1 < n_steps and not lonely(s - 1):
+            if 0 <= s - 1 < n_steps:
                 quantise(s - 1)
-            if 0 <= s - 3 < n_steps and lonely(s - 3):
-                quantise(s - 3)
             if s in vquants:
                 v_quantise(vquants[s][0], vquants[s][1])
             if s % MX_RUN == MX_RUN - 1 or s >= n_steps:

@@ -22,8 +22,7 @@ LN_GAMMA = math.log(0.96875)
 FLOPS = 2 * 2 * D * 3 * KG * KG * B
 
 MANUAL = True
-MX_LAG = 6
-MX_RUN = 2
+GROUP = 4
 
 UNITS = [(0, 0), (1, 0), (2, 0), (3, 0), (4, 0), (4, 1), (5, 0), (5, 1), (6, 0), (6, 1), (7, 0), (7, 1)]
 NU = len(UNITS)
@@ -35,7 +34,7 @@ def tile_retention_pa_t_kernel(tc, q, k, v, out):
         const = ctx.enter_context(tc.tile_pool(name="const", bufs=1))
         inputs = ctx.enter_context(tc.tile_pool(name="inputs", bufs=1))
         flipped = ctx.enter_context(tc.tile_pool(name="flipped", bufs=2))
-        work = ctx.enter_context(tc.tile_pool(name="work", bufs=3))
+        work = ctx.enter_context(tc.tile_pool(name="work", bufs=6))
         packed = ctx.enter_context(tc.tile_pool(name="packed", bufs=12))
         vpool = ctx.enter_context(tc.tile_pool(name="vpool", bufs=2))
         stage = ctx.enter_context(tc.tile_pool(name="stage", bufs=16))
@@ -103,21 +102,11 @@ def tile_retention_pa_t_kernel(tc, q, k, v, out):
                 words = src[b, g][:].bitcast(F32)
                 for n in range(PACK):
                     nc.tensor.transpose(bank[:, n, :], words[:, P * n : P * n + P], ident[:])
-                if src is q_sb:
-                    t = flipped.tile([P, KG, 2], BF16, tag=tag, name=tag)
-                    nc.scalar.copy(
-                        out=t[:].rearrange("w s e -> w (s e)").bitcast(F32).rearrange("w (p n) -> w p n", n=PACK),
-                        in_=bank[:].rearrange("w n p -> w p n"),
-                    )
-                else:
-                    t = flipped.tile([P, 2, KG], BF16, tag=tag, name=tag)
-                    nc.scalar.copy(
-                        out=t[:].rearrange("w e (p n) -> w e p n", n=PACK),
-                        in_=bank[:]
-                        .rearrange("w n p -> w (n p)")
-                        .bitcast(BF16)
-                        .rearrange("w (n p e) -> w e p n", n=PACK, e=2),
-                    )
+                t = flipped.tile([P, KG, 2], BF16, tag=tag, name=tag)
+                nc.scalar.copy(
+                    out=t[:].rearrange("w s e -> w (s e)").bitcast(F32).rearrange("w (p n) -> w p n", n=PACK),
+                    in_=bank[:].rearrange("w n p -> w p n"),
+                )
                 dst[b, g] = t
 
         vg, vc, vs = {}, {}, {}
@@ -152,7 +141,7 @@ def tile_retention_pa_t_kernel(tc, q, k, v, out):
                 for e in range(2):
                     nc.tensor.matmul(
                         out=bank[:, t, :],
-                        lhsT=kT[b, g][:, e, P * t : P * t + P],
+                        lhsT=kT[b, g][:, P * t : P * t + P, e],
                         rhs=qT[b, ib // PACK][:, cols, e],
                         start=(e == 0),
                         stop=(e == 1),
@@ -221,33 +210,33 @@ def tile_retention_pa_t_kernel(tc, q, k, v, out):
         flips, regroups, vquants = {}, {}, {}
         flips[2] = (0, 1)
         regroups[3] = (0, 1)
-        vquants[2] = (0, 0)
-        vquants[5] = (0, 1)
+        vquants[3] = [(0, 0)]
+        vquants[7] = [(0, 1)]
         for b in range(1, B):
             flips[NU * b - 6] = (b, 0)
             flips[NU * b - 2] = (b, 1)
             regroups[NU * b - 8] = (b, 0)
-            vquants[NU * b - 6] = (b, 0)
+            vquants[NU * b - 5] = vquants.get(NU * b - 5, []) + [(b, 0)]
             regroups[NU * b - 4] = (b, 1)
-            vquants[NU * b - 2] = (b, 1)
+            vquants[NU * b - 1] = vquants.get(NU * b - 1, []) + [(b, 1)]
 
         make_near()
         flip(0, 0)
         v_regroup(0, 0)
         make_far()
 
-        done = [0]
-        for s in range(n_steps + MX_LAG):
+        for s in range(n_steps + GROUP):
             if s < n_steps:
                 scores(s, flips.get(s))
                 mask_mult(s)
-            if 0 <= s - 1 < n_steps:
-                quantise(s - 1)
-            if s in vquants:
-                v_quantise(vquants[s][0], vquants[s][1])
-            if s % MX_RUN == MX_RUN - 1 or s >= n_steps:
-                while done[0] <= s - MX_LAG and done[0] < n_steps:
-                    mx(done[0])
-                    done[0] += 1
+            if s % GROUP == GROUP - 1:
+                if s < n_steps:
+                    for u in range(s - GROUP + 1, s + 1):
+                        quantise(u)
+                for b, g in vquants.get(s, []):
+                    v_quantise(b, g)
+                if s >= 2 * GROUP - 1:
+                    for u in range(s - 2 * GROUP + 1, s - GROUP + 1):
+                        mx(u)
             if s in regroups:
                 v_regroup(regroups[s][0], regroups[s][1])

@@ -11,6 +11,7 @@ U32 = mybir.dt.uint32
 U8 = mybir.dt.uint8
 FP8X4 = mybir.dt.float8_e4m3fn_x4
 MULT = mybir.AluOpType.mult
+ADD = mybir.AluOpType.add
 IS_GE = mybir.AluOpType.is_ge
 EXP = mybir.ActivationFunctionType.Exp
 
@@ -24,8 +25,9 @@ FLOPS = 2 * 2 * D * 3 * KG * KG * B
 MANUAL = True
 GROUP = 4
 
-UNITS = [(0, 0), (1, 0), (2, 0), (3, 0), (4, 0), (4, 1), (5, 0), (5, 1), (6, 0), (6, 1), (7, 0), (7, 1)]
+UNITS = [(0, 0), (1, 0), (2, 0), (3, 0), (4, 1), (5, 1), (4, 0), (5, 0), (6, 0), (6, 1), (7, 0), (7, 1)]
 NU = len(UNITS)
+MX_ORDER = [0, 1, 2, 3, 4, 6, 5, 7, 8, 9, 10, 11]
 
 
 def tile_retention_pa_t_kernel(tc, q, k, v, out):
@@ -162,12 +164,15 @@ def tile_retention_pa_t_kernel(tc, q, k, v, out):
                 weights = near[:, :, PACK - 1 - delta : PACK]
             else:
                 weights = far[:, :, 2 * PACK - 1 - delta : 3 * PACK - 1 - delta]
+            plane = work.tile([P, P, nv], BF16, tag="plane%d" % nv, name="plane") if nv <= 2 else t
             nc.vector.tensor_tensor(
-                out=t[:, :, 0:nv],
+                out=plane[:, :, 0:nv],
                 in0=banks[s][:, 0:nv, :].rearrange("p t c -> p c t"),
                 in1=weights,
                 op=MULT,
             )
+            if nv <= 2:
+                nc.gpsimd.tensor_scalar(out=t[:, :, 0:nv], in0=plane[:], scalar1=1.0, scalar2=0.0, op0=MULT, op1=ADD)
             grouped[s] = t
 
         def quantise(s):
@@ -186,14 +191,15 @@ def tile_retention_pa_t_kernel(tc, q, k, v, out):
             key = (b, ib) if split else (b, 2 * h)
             if key not in obank:
                 obank[key] = op.tile([P, 2, D], F32, tag="op", name="opbank")
-            last = g == ib // PACK
+            first = ib < PACK or g == (1 if ib < 6 else 0)
+            last = ib < PACK or g == (0 if ib < 6 else 1)
             nc.tensor.matmul_mx(
                 out=obank[key][:, ib % 2, :],
                 lhsT=codes[s][:].bitcast(FP8X4),
                 lhsT_scale=planes[s][:],
                 rhs=vc[b, g][:].bitcast(FP8X4),
                 rhs_scale=vs[b, g][:],
-                start=(g == 0),
+                start=first,
                 stop=last,
             )
             if last and split:
@@ -237,6 +243,6 @@ def tile_retention_pa_t_kernel(tc, q, k, v, out):
                     v_quantise(b, g)
                 if s >= 2 * GROUP - 1:
                     for u in range(s - 2 * GROUP + 1, s - GROUP + 1):
-                        mx(u)
+                        mx(u - u % NU + MX_ORDER[u % NU])
             if s in regroups:
                 v_regroup(regroups[s][0], regroups[s][1])

@@ -22,11 +22,10 @@ KG = P * PACK
 LN_GAMMA = math.log(0.96875)
 FLOPS = 2 * 2 * D * 3 * KG * KG * B
 
-MANUAL = True
-GROUP = 4
-
 UNITS = [(0, 0), (1, 0), (2, 0), (3, 0), (4, 1), (5, 1), (4, 0), (5, 0), (6, 0), (6, 1), (7, 0), (7, 1)]
 NU = len(UNITS)
+GROUP = 4
+KINDS = NU // GROUP
 MX_ORDER = [0, 1, 2, 3, 4, 6, 5, 7, 8, 9, 10, 11]
 
 
@@ -37,14 +36,13 @@ def tile_retention_pa_t_kernel(tc, q, k, v, out):
         inputs = ctx.enter_context(tc.tile_pool(name="inputs", bufs=1))
         flipped = ctx.enter_context(tc.tile_pool(name="flipped", bufs=2))
         work = ctx.enter_context(tc.tile_pool(name="work", bufs=6))
-        packed = ctx.enter_context(tc.tile_pool(name="packed", bufs=12))
+        packed = ctx.enter_context(tc.tile_pool(name="packed", bufs=4))
         vpool = ctx.enter_context(tc.tile_pool(name="vpool", bufs=2))
         stage = ctx.enter_context(tc.tile_pool(name="stage", bufs=16))
         tp = ctx.enter_context(tc.psum_pool(name="tp", bufs=2))
         sc = ctx.enter_context(tc.psum_pool(name="sc", bufs=4))
         op = ctx.enter_context(tc.psum_pool(name="op", bufs=2))
-        if MANUAL:
-            ctx.enter_context(tc.manual_schedule())
+        ctx.enter_context(tc.manual_schedule())
 
         q_sb, k_sb, v_sb = {}, {}, {}
         for b in range(B):
@@ -67,11 +65,14 @@ def tile_retention_pa_t_kernel(tc, q, k, v, out):
         masks.make_identity(nc, ident[:])
         xf = const.tile([P, P, PACK], F32, name="xf")
         nc.vector.tensor_copy(out=xf[:].rearrange("p c m -> p (c m)"), in_=xi[:])
-        gz = []
-        for delta in range(3):
-            z = const.tile([P, P, PACK], BF16, name="gz%d" % delta, align_bytes=64)
-            nc.vector.memset(z[:].rearrange("p c t -> p (c t)").bitcast(I32), 0)
-            gz.append(z)
+        grouped = []
+        for kind in range(KINDS):
+            z = const.tile([P, GROUP, P, PACK], BF16, name="grouped%d" % kind, align_bytes=64)
+            for i in range(GROUP):
+                ib, g = UNITS[GROUP * kind + i]
+                if ib - PACK * g < PACK - 1:
+                    nc.vector.memset(z[:, i].rearrange("p c t -> p (c t)").bitcast(I32), 0)
+            grouped.append(z)
         near = const.tile([P, P, PACK], F32, name="near")
         far = const.tile([P, P, 2 * PACK], F32, name="far")
 
@@ -132,7 +133,7 @@ def tile_retention_pa_t_kernel(tc, q, k, v, out):
 
         seq = [(b, ib, g) for b in range(B) for (ib, g) in UNITS]
         n_steps = len(seq)
-        banks, grouped, codes, planes, obank = {}, {}, {}, {}, {}
+        banks, codes, planes, obank = {}, {}, {}, {}
 
         def scores(s, mid):
             b, ib, g = seq[s]
@@ -156,32 +157,33 @@ def tile_retention_pa_t_kernel(tc, q, k, v, out):
             b, ib, g = seq[s]
             delta = ib - PACK * g
             nv = min(delta, PACK - 1) + 1
-            if delta < PACK - 1:
-                t = gz[delta]
-            else:
-                t = work.tile([P, P, PACK], BF16, tag="grouped", name="grouped", align_bytes=64)
+            t = grouped[s % NU // GROUP][:, s % GROUP]
             if delta < PACK:
                 weights = near[:, :, PACK - 1 - delta : PACK]
             else:
                 weights = far[:, :, 2 * PACK - 1 - delta : 3 * PACK - 1 - delta]
-            plane = work.tile([P, P, nv], BF16, tag="plane%d" % nv, name="plane") if nv <= 2 else t
+            if nv <= 2:
+                plane = work.tile([P, P, nv], BF16, tag="plane%d" % nv, name="plane")
+                dst = plane[:]
+            else:
+                dst = t[:, :, 0:nv]
             nc.vector.tensor_tensor(
-                out=plane[:, :, 0:nv],
+                out=dst,
                 in0=banks[s][:, 0:nv, :].rearrange("p t c -> p c t"),
                 in1=weights,
                 op=MULT,
             )
             if nv <= 2:
                 nc.gpsimd.tensor_scalar(out=t[:, :, 0:nv], in0=plane[:], scalar1=1.0, scalar2=0.0, op0=MULT, op1=ADD)
-            grouped[s] = t
 
-        def quantise(s):
-            codes[s] = packed.tile([P, P], U32, tag="codes", name="codes", align_bytes=64)
-            planes[s] = packed.tile([P, P], U8, tag="planes", name="planes", align_bytes=64)
+        def quantise(j, i, n):
+            if j not in codes:
+                codes[j] = packed.tile([P, GROUP * P], U32, tag="codes", name="codes", align_bytes=64)
+                planes[j] = packed.tile([P, GROUP * P], U8, tag="planes", name="planes", align_bytes=64)
             nc.vector.quantize_mx(
-                out=codes[s][:].bitcast(FP8X4),
-                scales=planes[s][:],
-                in_=grouped[s][:].rearrange("p c t -> p (c t)"),
+                out=codes[j][:, P * i : P * i + P * n].bitcast(FP8X4),
+                scales=planes[j][:, P * i : P * i + P * n],
+                in_=grouped[j % KINDS][:, i : i + n].rearrange("p u c t -> p (u c t)"),
             )
 
         def mx(s):
@@ -195,8 +197,8 @@ def tile_retention_pa_t_kernel(tc, q, k, v, out):
             last = ib < PACK or g == (0 if ib < 6 else 1)
             nc.tensor.matmul_mx(
                 out=obank[key][:, ib % 2, :],
-                lhsT=codes[s][:].bitcast(FP8X4),
-                lhsT_scale=planes[s][:],
+                lhsT=codes[s // GROUP][:, P * (s % GROUP) : P * (s % GROUP) + P].bitcast(FP8X4),
+                lhsT_scale=planes[s // GROUP][:, P * (s % GROUP) : P * (s % GROUP) + P],
                 rhs=vc[b, g][:].bitcast(FP8X4),
                 rhs_scale=vs[b, g][:],
                 start=first,
@@ -212,6 +214,10 @@ def tile_retention_pa_t_kernel(tc, q, k, v, out):
                 nc.sync.dma_start(
                     out=out[b, 2 * P * h : 2 * P * h + 2 * P, :].rearrange("(n c) d -> c n d", c=P), in_=o[:]
                 )
+
+        def mx_group(j):
+            for u in range(GROUP * j, GROUP * j + GROUP):
+                mx(u - u % NU + MX_ORDER[u % NU])
 
         flips, regroups, vquants = {}, {}, {}
         flips[2] = (0, 1)
@@ -231,18 +237,21 @@ def tile_retention_pa_t_kernel(tc, q, k, v, out):
         v_regroup(0, 0)
         make_far()
 
-        for s in range(n_steps + GROUP):
-            if s < n_steps:
-                scores(s, flips.get(s))
-                mask_mult(s)
-            if s % GROUP == GROUP - 1:
-                if s < n_steps:
-                    for u in range(s - GROUP + 1, s + 1):
-                        quantise(u)
-                for b, g in vquants.get(s, []):
-                    v_quantise(b, g)
-                if s >= 2 * GROUP - 1:
-                    for u in range(s - 2 * GROUP + 1, s - GROUP + 1):
-                        mx(u - u % NU + MX_ORDER[u % NU])
+        n_groups = n_steps // GROUP
+        for s in range(n_steps):
+            j, i = divmod(s, GROUP)
+            scores(s, flips.get(s))
+            mask_mult(s)
+            if i == 0 and j > 0:
+                quantise(j - 1, 0, GROUP)
+            if j == n_groups - 1 and i > 0:
+                quantise(j, i - 1, 1)
+            for b, g in vquants.get(s, []):
+                v_quantise(b, g)
+            if i == 1 and j > 1:
+                mx_group(j - 2)
             if s in regroups:
                 v_regroup(regroups[s][0], regroups[s][1])
+        quantise(n_groups - 1, GROUP - 1, 1)
+        mx_group(n_groups - 2)
+        mx_group(n_groups - 1)

@@ -99,12 +99,16 @@ def tile_retention_pa_t_kernel(tc, q, k, v, out):
 
         qT, kT = {}, {}
 
-        def flip(b, g):
-            for src, dst, tag in ((q_sb, qT, "qT%d" % g), (k_sb, kT, "kT%d" % g)):
-                bank = tp.tile([P, PACK, P], F32, tag="tp", name="tpbank")
-                words = src[b, g][:].bitcast(F32)
-                for n in range(PACK):
-                    nc.tensor.transpose(bank[:, n, :], words[:, P * n : P * n + P], ident[:])
+        flip_bank = {}
+
+        def flip_part(b, g, i):
+            src, dst, tag = (q_sb, qT, "qT%d" % g) if i < PACK else (k_sb, kT, "kT%d" % g)
+            n = i % PACK
+            if n == 0:
+                flip_bank[0] = tp.tile([P, PACK, P], F32, tag="tp", name="tpbank")
+            bank = flip_bank[0]
+            nc.tensor.transpose(bank[:, n, :], src[b, g][:].bitcast(F32)[:, P * n : P * n + P], ident[:])
+            if n == PACK - 1:
                 t = flipped.tile([P, KG, 2], BF16, tag=tag, name=tag)
                 nc.scalar.copy(
                     out=t[:].rearrange("w s e -> w (s e)").bitcast(F32).rearrange("w (p n) -> w p n", n=PACK),
@@ -135,7 +139,16 @@ def tile_retention_pa_t_kernel(tc, q, k, v, out):
         n_steps = len(seq)
         banks, codes, planes, obank = {}, {}, {}, {}
 
-        def scores(s, mid):
+        flips = {}
+        pairs = sum(min(ib - PACK * g, PACK - 1) + 1 for ib, g in UNITS)
+        for i in range(2 * PACK):
+            flips[i] = (0, 1, i)
+            for b in range(1, B):
+                flips[pairs * (b - 1) + 2 * i + (11 if b == 1 else 1)] = (b, 0, i)
+                flips[pairs * (b - 1) + (27 + i if b == 1 else 17 + 2 * i)] = (b, 1, i)
+        pair = [0]
+
+        def scores(s):
             b, ib, g = seq[s]
             nv = min(ib - PACK * g, PACK - 1) + 1
             bank = sc.tile([P, PACK, P], F32, tag="sc", name="scbank")
@@ -149,8 +162,9 @@ def tile_retention_pa_t_kernel(tc, q, k, v, out):
                         start=(e == 0),
                         stop=(e == 1),
                     )
-                if t == 0 and mid is not None:
-                    flip(mid[0], mid[1])
+                if pair[0] in flips:
+                    flip_part(*flips[pair[0]])
+                pair[0] += 1
             banks[s] = bank
 
         def mask_mult(s):
@@ -219,28 +233,26 @@ def tile_retention_pa_t_kernel(tc, q, k, v, out):
             for u in range(GROUP * j, GROUP * j + GROUP):
                 mx(u - u % NU + MX_ORDER[u % NU])
 
-        flips, regroups, vquants = {}, {}, {}
-        flips[2] = (0, 1)
+        regroups, vquants = {}, {}
         regroups[3] = (0, 1)
         vquants[3] = [(0, 0)]
         vquants[7] = [(0, 1)]
         for b in range(1, B):
-            flips[NU * b - 6] = (b, 0)
-            flips[NU * b - 2] = (b, 1)
             regroups[NU * b - 8] = (b, 0)
             vquants[NU * b - 5] = vquants.get(NU * b - 5, []) + [(b, 0)]
             regroups[NU * b - 4] = (b, 1)
             vquants[NU * b - 1] = vquants.get(NU * b - 1, []) + [(b, 1)]
 
         make_near()
-        flip(0, 0)
+        for i in range(2 * PACK):
+            flip_part(0, 0, i)
         v_regroup(0, 0)
         make_far()
 
         n_groups = n_steps // GROUP
         for s in range(n_steps):
             j, i = divmod(s, GROUP)
-            scores(s, flips.get(s))
+            scores(s)
             mask_mult(s)
             if i == 0 and j > 0:
                 quantise(j - 1, 0, GROUP)

import math
from contextlib import ExitStack

import concourse.masks as masks
import concourse.mybir as mybir

F32 = mybir.dt.float32
BF16 = mybir.dt.bfloat16
I32 = mybir.dt.int32
U32 = mybir.dt.uint32
U8 = mybir.dt.uint8
FP8X4 = mybir.dt.float8_e4m3fn_x4
MULT = mybir.AluOpType.mult
ADD = mybir.AluOpType.add
IS_GE = mybir.AluOpType.is_ge
EXP = mybir.ActivationFunctionType.Exp

B, S, D = 8, 1024, 256
P = 128
PACK = 4
KG = P * PACK
LN_GAMMA = math.log(0.96875)
FLOPS = 2 * 2 * D * 3 * KG * KG * B

UNITS = [(0, 0), (1, 0), (2, 0), (3, 0), (4, 1), (5, 1), (4, 0), (5, 0), (6, 0), (6, 1), (7, 0), (7, 1)]
NU = len(UNITS)
GROUP = 4
KINDS = NU // GROUP
MX_ORDER = [0, 1, 2, 3, 4, 6, 5, 7, 8, 9, 10, 11]


def tile_retention_pa_t_kernel(tc, q, k, v, out):
    nc = tc.nc
    with ExitStack() as ctx:
        const = ctx.enter_context(tc.tile_pool(name="const", bufs=1))
        inputs = ctx.enter_context(tc.tile_pool(name="inputs", bufs=1))
        flipped = ctx.enter_context(tc.tile_pool(name="flipped", bufs=2))
        work = ctx.enter_context(tc.tile_pool(name="work", bufs=6))
        packed = ctx.enter_context(tc.tile_pool(name="packed", bufs=4))
        vpool = ctx.enter_context(tc.tile_pool(name="vpool", bufs=2))
        stage = ctx.enter_context(tc.tile_pool(name="stage", bufs=16))
        tp = ctx.enter_context(tc.psum_pool(name="tp", bufs=2))
        sc = ctx.enter_context(tc.psum_pool(name="sc", bufs=4))
        op = ctx.enter_context(tc.psum_pool(name="op", bufs=2))
        ctx.enter_context(tc.manual_schedule())

        q_sb, k_sb, v_sb = {}, {}, {}
        for b in range(B):
            for g in range(2):
                rows = slice(KG * g, KG * g + KG)
                q_sb[b, g] = inputs.tile([P, PACK * D], BF16, name="q%d_%d" % (b, g))
                nc.sync.dma_start(out=q_sb[b, g][:], in_=q[b, rows, :].rearrange("(p n) d -> p (n d)", n=PACK))
                k_sb[b, g] = inputs.tile([P, PACK * D], BF16, name="k%d_%d" % (b, g))
                nc.sync.dma_start(out=k_sb[b, g][:], in_=k[b, rows, :].rearrange("(p n) d -> p (n d)", n=PACK))
                v_sb[b, g] = inputs.tile([P, PACK, D], BF16, name="v%d_%d" % (b, g))
                nc.sync.dma_start(out=v_sb[b, g][:], in_=v[b, rows, :].rearrange("(t p) d -> p t d", p=P))

        cold = const.tile([P, 1], F32, name="cold")
        warm = const.tile([P, 1], F32, name="warm")
        nc.vector.memset(cold[:], 0.0)
        nc.scalar.activation(out=warm[:], in_=cold[:], func=EXP, bias=0.0, scale=1.0)
        xi = const.tile([P, P * PACK], I32, name="xi")
        nc.gpsimd.iota(out=xi[:], pattern=[[1, P], [-P, PACK]], base=P * (PACK - 1), channel_multiplier=-1)
        ident = const.tile([P, P], F32, name="ident")
        masks.make_identity(nc, ident[:])
        xf = const.tile([P, P, PACK], F32, name="xf")
        nc.vector.tensor_copy(out=xf[:].rearrange("p c m -> p (c m)"), in_=xi[:])
        grouped = []
        for kind in range(KINDS):
            z = const.tile([P, GROUP, P, PACK], BF16, name="grouped%d" % kind, align_bytes=64)
            for i in range(GROUP):
                ib, g = UNITS[GROUP * kind + i]
                if ib - PACK * g < PACK - 1:
                    nc.vector.memset(z[:, i].rearrange("p c t -> p (c t)").bitcast(I32), 0)
            grouped.append(z)
        near = const.tile([P, P, PACK], F32, name="near")
        far = const.tile([P, P, 2 * PACK], F32, name="far")

        def make_near():
            nc.scalar.activation(out=near[:], in_=xf[:], func=EXP, bias=0.0, scale=LN_GAMMA)
            nc.vector.scalar_tensor_tensor(
                out=near[:, :, PACK - 1],
                in0=xf[:, :, PACK - 1],
                scalar=0.0,
                in1=near[:, :, PACK - 1],
                op0=IS_GE,
                op1=MULT,
            )

        def make_far():
            for half in range(2):
                nc.scalar.activation(
                    out=far[:, :, PACK * half : PACK * half + PACK],
                    in_=xf[:],
                    func=EXP,
                    bias=(1 - half) * KG * LN_GAMMA,
                    scale=LN_GAMMA,
                )

        qT, kT = {}, {}

        flip_bank = {}

        def flip_part(b, g, i):
            src, dst, tag = (q_sb, qT, "qT%d" % g) if i < PACK else (k_sb, kT, "kT%d" % g)
            n = i % PACK
            if n == 0:
                flip_bank[0] = tp.tile([P, PACK, P], F32, tag="tp", name="tpbank")
            bank = flip_bank[0]
            nc.tensor.transpose(bank[:, n, :], src[b, g][:].bitcast(F32)[:, P * n : P * n + P], ident[:])
            if n == PACK - 1:
                t = flipped.tile([P, KG, 2], BF16, tag=tag, name=tag)
                nc.scalar.copy(
                    out=t[:].rearrange("w s e -> w (s e)").bitcast(F32).rearrange("w (p n) -> w p n", n=PACK),
                    in_=bank[:].rearrange("w n p -> w p n"),
                )
                dst[b, g] = t

        vg, vc, vs = {}, {}, {}

        def v_regroup(b, g):
            t = vpool.tile([P, D, PACK], BF16, tag="vg%d" % g, name="vg", align_bytes=64)
            nc.scalar.copy(
                out=t[:].rearrange("p (c i) t -> p c t i", i=4),
                in_=v_sb[b, g][:].rearrange("p t (c i) -> p c t i", i=4),
            )
            vg[b, g] = t

        def v_quantise(b, g):
            vc[b, g] = vpool.tile([P, D], U32, tag="vc%d" % g, name="vc", align_bytes=64)
            vs[b, g] = vpool.tile([P, D], U8, tag="vs%d" % g, name="vs", align_bytes=64)
            nc.vector.quantize_mx(
                out=vc[b, g][:].bitcast(FP8X4),
                scales=vs[b, g][:],
                in_=vg[b, g][:].rearrange("p d t -> p (d t)"),
            )

        seq = [(b, ib, g) for b in range(B) for (ib, g) in UNITS]
        n_steps = len(seq)
        banks, codes, planes, obank = {}, {}, {}, {}

        flips = {}
        pairs = sum(min(ib - PACK * g, PACK - 1) + 1 for ib, g in UNITS)
        for i in range(2 * PACK):
            flips[i] = (0, 1, i)
            for b in range(1, B):
                flips[pairs * (b - 1) + 2 * i + (11 if b == 1 else 1)] = (b, 0, i)
                flips[pairs * (b - 1) + (27 + i if b == 1 else 17 + 2 * i)] = (b, 1, i)
        pair = [0]

        def scores(s):
            b, ib, g = seq[s]
            nv = min(ib - PACK * g, PACK - 1) + 1
            bank = sc.tile([P, PACK, P], F32, tag="sc", name="scbank")
            cols = slice(P * (ib % PACK), P * (ib % PACK) + P)
            for t in range(nv):
                for e in range(2):
                    nc.tensor.matmul(
                        out=bank[:, t, :],
                        lhsT=kT[b, g][:, P * t : P * t + P, e],
                        rhs=qT[b, ib // PACK][:, cols, e],
                        start=(e == 0),
                        stop=(e == 1),
                    )
                if pair[0] in flips:
                    flip_part(*flips[pair[0]])
                pair[0] += 1
            banks[s] = bank

        def mask_mult(s):
            b, ib, g = seq[s]
            delta = ib - PACK * g
            nv = min(delta, PACK - 1) + 1
            t = grouped[s % NU // GROUP][:, s % GROUP]
            if delta < PACK:
                weights = near[:, :, PACK - 1 - delta : PACK]
            else:
                weights = far[:, :, 2 * PACK - 1 - delta : 3 * PACK - 1 - delta]
            if nv <= 2:
                plane = work.tile([P, P, nv], BF16, tag="plane%d" % nv, name="plane")
                dst = plane[:]
            else:
                dst = t[:, :, 0:nv]
            nc.vector.tensor_tensor(
                out=dst,
                in0=banks[s][:, 0:nv, :].rearrange("p t c -> p c t"),
                in1=weights,
                op=MULT,
            )
            if nv <= 2:
                nc.gpsimd.tensor_scalar(out=t[:, :, 0:nv], in0=plane[:], scalar1=1.0, scalar2=0.0, op0=MULT, op1=ADD)

        def quantise(j, i, n):
            if j not in codes:
                codes[j] = packed.tile([P, GROUP * P], U32, tag="codes", name="codes", align_bytes=64)
                planes[j] = packed.tile([P, GROUP * P], U8, tag="planes", name="planes", align_bytes=64)
            nc.vector.quantize_mx(
                out=codes[j][:, P * i : P * i + P * n].bitcast(FP8X4),
                scales=planes[j][:, P * i : P * i + P * n],
                in_=grouped[j % KINDS][:, i : i + n].rearrange("p u c t -> p (u c t)"),
            )

        def mx(s):
            b, ib, g = seq[s]
            h = ib // 2
            split = b == B - 1 and h == 3
            key = (b, ib) if split else (b, 2 * h)
            if key not in obank:
                obank[key] = op.tile([P, 2, D], F32, tag="op", name="opbank")
            first = ib < PACK or g == (1 if ib < 6 else 0)
            last = ib < PACK or g == (0 if ib < 6 else 1)
            nc.tensor.matmul_mx(
                out=obank[key][:, ib % 2, :],
                lhsT=codes[s // GROUP][:, P * (s % GROUP) : P * (s % GROUP) + P].bitcast(FP8X4),
                lhsT_scale=planes[s // GROUP][:, P * (s % GROUP) : P * (s % GROUP) + P],
                rhs=vc[b, g][:].bitcast(FP8X4),
                rhs_scale=vs[b, g][:],
                start=first,
                stop=last,
            )
            if last and split:
                o = stage.tile([P, 2, D], F32, tag="o", name="o")
                nc.scalar.copy(out=o[:, 0, :], in_=obank[key][:, ib % 2, :])
                nc.sync.dma_start(out=out[b, P * ib : P * ib + P, :], in_=o[:, 0, :])
            elif last and ib % 2 == 1:
                o = stage.tile([P, 2, D], F32, tag="o", name="o")
                nc.scalar.copy(out=o[:], in_=obank[key][:])
                nc.sync.dma_start(
                    out=out[b, 2 * P * h : 2 * P * h + 2 * P, :].rearrange("(n c) d -> c n d", c=P), in_=o[:]
                )

        def mx_group(j):
            for u in range(GROUP * j, GROUP * j + GROUP):
                mx(u - u % NU + MX_ORDER[u % NU])

        regroups, vquants = {}, {}
        regroups[3] = (0, 1)
        vquants[3] = [(0, 0)]
        vquants[7] = [(0, 1)]
        for b in range(1, B):
            regroups[NU * b - 8] = (b, 0)
            vquants[NU * b - 5] = vquants.get(NU * b - 5, []) + [(b, 0)]
            regroups[NU * b - 4] = (b, 1)
            vquants[NU * b - 1] = vquants.get(NU * b - 1, []) + [(b, 1)]

        make_near()
        for i in range(2 * PACK):
            flip_part(0, 0, i)
        v_regroup(0, 0)
        make_far()

        n_groups = n_steps // GROUP
        for s in range(n_steps):
            j, i = divmod(s, GROUP)
            scores(s)
            mask_mult(s)
            if i == 0 and j > 0:
                quantise(j - 1, 0, GROUP)
            if j == n_groups - 1 and i > 0:
                quantise(j, i - 1, 1)
            for b, g in vquants.get(s, []):
                v_quantise(b, g)
            if i == 1 and j > 1:
                mx_group(j - 2)
            if s in regroups:
                v_regroup(regroups[s][0], regroups[s][1])
        quantise(n_groups - 1, GROUP - 1, 1)
        mx_group(n_groups - 2)
        mx_group(n_groups - 1)
